import numpy as np
import ml_dtypes


def mxq(x, axis, fmt="e4m3"):
    dtype, down = {"e4m3": (ml_dtypes.float8_e4m3fn, 7), "e5m2": (ml_dtypes.float8_e5m2, 14)}[fmt]
    v = np.moveaxis(np.asarray(x, np.float32).astype(ml_dtypes.bfloat16).astype(np.float64), axis, -1)
    blocks = v.reshape(v.shape[:-1] + (-1, 32))
    amax = np.abs(blocks).max(-1, keepdims=True)
    byte = np.maximum(np.where(amax > 0, np.frexp(amax)[1] - 1 + 127, 0) - down, 1)
    scale = np.exp2(byte - 127.0)
    codes = (blocks / scale).astype(np.float32).astype(dtype).astype(np.float64)
    return np.moveaxis((codes * scale).reshape(v.shape), -1, axis)


WIDE = False


def mx_kscale(k):
    if not WIDE:
        return np.ones(k)
    levels = np.array([10, -10, 5, -5, 0])
    a = np.random.permutation(np.resize(levels, k // 512 * 4)).reshape(k // 512, 4)
    idx = np.arange(k)
    return np.exp2(a[idx // 512, idx % 128 // 32])


BF16 = ml_dtypes.bfloat16


def bf(x):
    return np.asarray(x, np.float32).astype(BF16)


def f64(x):
    return np.asarray(x).astype(np.float64)


B, NI, NK, NJ, C_Z, C_H = 1, 128, 8192, 128, 128, 8
EPS = 1e-5
KEEP = 0.85


def layer_norm(x, w, b):
    mu = x.mean(-1, keepdims=True)
    var = ((x - mu) ** 2).mean(-1, keepdims=True)
    return (x - mu) / np.sqrt(var + EPS) * w + b


def setup_inputs():
    s = mx_kscale(NK)
    return {"a_gated": bf(np.random.standard_normal((B, NI, NK, C_H)) * 0.55 * s[None, None, :, None]),
            "b_gated": bf(np.random.standard_normal((B, NK, NJ, C_H)) * 0.55 / s[None, :, None, None]),
            "mask_ik": bf(np.random.random((B, NI, NK)) < KEEP),
            "mask_kj": bf(np.random.random((B, NK, NJ)) < KEEP),
            "ln_out_w": bf(1.0 + 0.1 * np.random.standard_normal(C_H)),
            "ln_out_b": bf(0.1 * np.random.standard_normal(C_H))}


def reference(a_gated, b_gated, mask_ik, mask_kj, ln_out_w, ln_out_b):
    a = f64(mask_ik)[..., None] * f64(a_gated)
    b = f64(mask_kj)[..., None] * f64(b_gated)
    at = a.transpose(0, 3, 1, 2)
    bt = b.transpose(0, 3, 1, 2)
    x = (mxq(at, 3, "e4m3") @ mxq(bt, 2, "e4m3")).transpose(0, 2, 3, 1)
    return layer_norm(x, f64(ln_out_w), f64(ln_out_b))

@@ -1,0 +1,223 @@
+from contextlib import ExitStack
+
+import concourse.mybir as mybir
+from concourse.masks import make_identity
+
+F32 = mybir.dt.float32
+BF16 = mybir.dt.bfloat16
+I32 = mybir.dt.int32
+U32 = mybir.dt.uint32
+U8 = mybir.dt.uint8
+FP8X4 = mybir.dt.float8_e4m3fn_x4
+ALU = mybir.AluOpType
+ACT = mybir.ActivationFunctionType
+
+P = 128
+NI = 128
+NJ = 128
+NK = 8192
+CH = 8
+PACK = 4
+K_PASS = P * PACK
+PASSES = NK // K_PASS
+ROUND = 4
+ROUNDS = PASSES // ROUND
+PAIRS = CH // 2
+HALF = CH // 2
+J_SCALAR = 88
+EPS = 1e-5
+
+FLOPS = 2 * NI * NJ * NK * CH
+
+
+def tile_trianglemultiplicativeupdate_pa_k_kernel(
+    tc, a_gated, b_gated, mask_ik, mask_kj, ln_out_w, ln_out_b, out
+):
+    nc = tc.nc
+    a_rows = a_gated[0].rearrange("i (g k) d -> g i (k d)", k=K_PASS)
+    b_rows = b_gated[0].rearrange("(g t p) j d -> g p t (j d)", t=PACK, p=P)
+    mask_a_rows = mask_ik[0].rearrange("i (r k) -> r i k", r=ROUNDS)
+    mask_b_rows = mask_kj[0].rearrange("(r c p) j -> r p c j", r=ROUNDS, p=P)
+
+    with ExitStack() as ctx:
+        const = ctx.enter_context(tc.tile_pool(name="const", bufs=1))
+        mask_pool = ctx.enter_context(tc.tile_pool(name="mask_pool", bufs=2))
+        keeps = ctx.enter_context(tc.tile_pool(name="keeps", bufs=1))
+        loads = ctx.enter_context(tc.tile_pool(name="loads", bufs=3))
+        grouped = ctx.enter_context(tc.tile_pool(name="grouped", bufs=2))
+        quant = ctx.enter_context(tc.tile_pool(name="quant", bufs=2))
+        norm = ctx.enter_context(tc.tile_pool(name="norm", bufs=1))
+        turn_psum = ctx.enter_context(tc.psum_pool(name="turn_psum", bufs=6))
+        acc_psum = ctx.enter_context(tc.psum_pool(name="acc_psum", bufs=1))
+
+        eps_col = const.tile([P, 1], F32)
+        nc.vector.memset(eps_col[:], EPS)
+        warm = const.tile([P, 1], F32)
+        nc.scalar.activation(out=warm[:], in_=eps_col[:], func=ACT.Sqrt)
+        ident = const.tile([P, P], F32)
+        make_identity(nc, ident[:])
+        gain_bf = const.tile([P, CH], BF16)
+        nc.gpsimd.dma_start(out=gain_bf[:], in_=ln_out_w.partition_broadcast(P))
+        bias_bf = const.tile([P, CH], BF16)
+        nc.gpsimd.dma_start(out=bias_bf[:], in_=ln_out_b.partition_broadcast(P))
+        gain = const.tile([P, CH], F32)
+        nc.gpsimd.tensor_copy(out=gain[:], in_=gain_bf[:])
+        bias = const.tile([P, CH], F32)
+        nc.gpsimd.tensor_copy(out=bias[:], in_=bias_bf[:])
+
+        x_sum = const.tile([P, CH, NJ], F32)
+        x = norm.tile([P, NJ, CH], F32)
+
+        for r in range(ROUNDS):
+            mask_a = mask_pool.tile([P, ROUND * K_PASS], BF16)
+            nc.sync.dma_start(out=mask_a[:], in_=mask_a_rows[r])
+            mask_b = mask_pool.tile([P, ROUND * PACK, NJ], BF16)
+            nc.sync.dma_start(out=mask_b[:], in_=mask_b_rows[r])
+            keep_a = keeps.tile([P, ROUND * K_PASS], I32)
+            nc.vector.tensor_scalar(
+                out=keep_a[:], in0=mask_a[:], scalar1=-1.0, scalar2=None, op0=ALU.mult
+            )
+            keep_b = keeps.tile([P, ROUND * PACK, J_SCALAR], I32)
+            nc.vector.tensor_scalar(
+                out=keep_b[:], in0=mask_b[:, :, :J_SCALAR], scalar1=-1.0, scalar2=None, op0=ALU.mult
+            )
+
+            a_codes = quant.tile([P, ROUND, CH * NI], U32, align_bytes=64)
+            a_scales = quant.tile([P, ROUND, CH * NI], U8, align_bytes=64)
+            b_codes = quant.tile([P, ROUND, CH * NJ], U32, align_bytes=64)
+            b_scales = quant.tile([P, ROUND, CH * NJ], U8, align_bytes=64)
+
+            for c in range(ROUND):
+                g = r * ROUND + c
+                a_nat = loads.tile([P, K_PASS * CH], BF16)
+                nc.sync.dma_start(out=a_nat[:], in_=a_rows[g])
+                b_nat = loads.tile([P, PACK, NJ, CH], BF16)
+                nc.sync.dma_start(out=b_nat[:].rearrange("p t j d -> p t (j d)"), in_=b_rows[g])
+
+                a_words = a_nat[:].bitcast(I32).rearrange("p (k u) -> p k u", u=PAIRS)
+                nc.vector.tensor_tensor(
+                    out=a_words,
+                    in0=a_words,
+                    in1=keep_a[:, c * K_PASS : (c + 1) * K_PASS]
+                    .unsqueeze(2)
+                    .to_broadcast([P, K_PASS, PAIRS]),
+                    op=ALU.bitwise_and,
+                )
+                a_f32 = a_nat[:].bitcast(F32).rearrange("p (t k u) -> p t k u", t=PACK, u=PAIRS)
+                a_grouped = grouped.tile([P, CH, NI, PACK], BF16, align_bytes=64)
+                for u in range(PAIRS):
+                    turned = turn_psum.tile([P, PACK * NI], F32)
+                    for t in range(PACK):
+                        nc.tensor.transpose(
+                            turned[:, t * NI : (t + 1) * NI], a_f32[:, t, :, u], ident[:]
+                        )
+                    nc.scalar.copy(
+                        out=a_grouped[:, 2 * u : 2 * u + 2, :, :],
+                        in_=turned[:].bitcast(BF16).rearrange("p (t i e) -> p e i t", t=PACK, e=2),
+                    )
+
+                b_words = (
+                    b_nat[:]
+                    .rearrange("p t j d -> p (t j d)")
+                    .bitcast(I32)
+                    .rearrange("p (t j u) -> p t j u", t=PACK, u=PAIRS)
+                )
+                nc.vector.tensor_tensor(
+                    out=b_words[:, :, :J_SCALAR, :],
+                    in0=b_words[:, :, :J_SCALAR, :],
+                    in1=keep_b[:, c * PACK : (c + 1) * PACK, :]
+                    .unsqueeze(3)
+                    .to_broadcast([P, PACK, J_SCALAR, PAIRS]),
+                    op=ALU.bitwise_and,
+                )
+                b_grouped = grouped.tile([P, CH, NJ, PACK], BF16, align_bytes=64)
+                for h in range(CH // HALF):
+                    ch = slice(h * HALF, (h + 1) * HALF)
+                    nc.scalar.copy(
+                        out=b_grouped[:, ch, :J_SCALAR, :].rearrange("p d j t -> p j d t"),
+                        in_=b_nat[:, :, :J_SCALAR, ch].rearrange("p t j d -> p j d t"),
+                    )
+                    nc.vector.tensor_tensor(
+                        out=b_grouped[:, ch, J_SCALAR:, :].rearrange("p d j t -> p j d t"),
+                        in0=b_nat[:, :, J_SCALAR:, ch].rearrange("p t j d -> p j d t"),
+                        in1=mask_b[:, c * PACK : (c + 1) * PACK, J_SCALAR:]
+                        .rearrange("p t j -> p j t")
+                        .unsqueeze(2)
+                        .to_broadcast([P, NJ - J_SCALAR, HALF, PACK]),
+                        op=ALU.mult,
+                    )
+
+                nc.vector.quantize_mx(
+                    out=b_codes[:, c, :].bitcast(FP8X4),
+                    scales=b_scales[:, c, :],
+                    in_=b_grouped[:].rearrange("p d j t -> p (d j t)"),
+                )
+                nc.vector.quantize_mx(
+                    out=a_codes[:, c, :].bitcast(FP8X4),
+                    scales=a_scales[:, c, :],
+                    in_=a_grouped[:].rearrange("p d i t -> p (d i t)"),
+                )
+
+            for h in range(CH // HALF):
+                ch = slice(h * HALF, (h + 1) * HALF)
+                acc = acc_psum.tile([P, HALF, NJ], F32, tag="acc%d" % h)
+                for q in range(HALF):
+                    cols = slice((h * HALF + q) * P, (h * HALF + q + 1) * P)
+                    for c in range(ROUND):
+                        nc.tensor.matmul_mx(
+                            out=acc[:, q, :],
+                            lhsT=a_codes[:, c, cols].bitcast(FP8X4),
+                            lhsT_scale=a_scales[:, c, cols],
+                            rhs=b_codes[:, c, cols].bitcast(FP8X4),
+                            rhs_scale=b_scales[:, c, cols],
+                            start=(c == 0),
+                            stop=(c == ROUND - 1),
+                        )
+                if r == 0:
+                    nc.scalar.copy(out=x_sum[:, ch, :], in_=acc[:])
+                elif r < ROUNDS - 1:
+                    nc.vector.tensor_tensor(
+                        out=x_sum[:, ch, :], in0=acc[:], in1=x_sum[:, ch, :], op=ALU.add
+                    )
+                else:
+                    nc.vector.tensor_tensor(
+                        out=x[:, :, ch],
+                        in0=acc[:].rearrange("p d j -> p j d"),
+                        in1=x_sum[:, ch, :].rearrange("p d j -> p j d"),
+                        op=ALU.add,
+                    )
+
+        total = norm.tile([P, NJ], F32)
+        nc.vector.tensor_reduce(out=total[:], in_=x[:], axis=mybir.AxisListType.X, op=ALU.add)
+        centred = norm.tile([P, NJ, CH], F32)
+        nc.vector.scalar_tensor_tensor(
+            out=centred[:],
+            in0=total[:].unsqueeze(2).to_broadcast([P, NJ, CH]),
+            scalar=-1.0 / CH,
+            in1=x[:],
+            op0=ALU.mult,
+            op1=ALU.add,
+        )
+        squares = norm.tile([P, NJ, CH], F32)
+        nc.scalar.activation(out=squares[:], in_=centred[:], func=ACT.Square)
+        weighted = norm.tile([P, NJ, CH], F32)
+        nc.gpsimd.tensor_tensor(
+            out=weighted[:],
+            in0=centred[:],
+            in1=gain[:].unsqueeze(1).to_broadcast([P, NJ, CH]),
+            op=ALU.mult,
+        )
+        spread = norm.tile([P, NJ], F32)
+        nc.vector.tensor_reduce(out=spread[:], in_=squares[:], axis=mybir.AxisListType.X, op=ALU.add)
+        std = norm.tile([P, NJ], F32)
+        nc.scalar.activation(out=std[:], in_=spread[:], func=ACT.Sqrt, bias=eps_col[:], scale=1.0 / CH)
+        rstd = norm.tile([P, NJ], F32)
+        nc.vector.reciprocal(out=rstd[:], in_=std[:])
+        y = norm.tile([P, NJ, CH], F32)
+        nc.vector.tensor_tensor(
+            out=y[:], in0=weighted[:], in1=rstd[:].unsqueeze(2).to_broadcast([P, NJ, CH]), op=ALU.mult
+        )
+        nc.vector.tensor_tensor(
+            out=y[:], in0=y[:], in1=bias[:].unsqueeze(1).to_broadcast([P, NJ, CH]), op=ALU.add
+        )
+        nc.sync.dma_start(out=out[0].rearrange("i j d -> i (j d)"), in_=y[:].rearrange("p j d -> p (j d)"))

@@ -24,7 +24,7 @@ ROUND = 4
 ROUNDS = PASSES // ROUND
 PAIRS = CH // 2
 HALF = CH // 2
-J_SCALAR = 88
+J_SCALAR = 64
 EPS = 1e-5
 
 FLOPS = 2 * NI * NJ * NK * CH
@@ -67,6 +67,7 @@ def tile_trianglemultiplicativeupdate_pa_k_kernel(
 
         x_sum = const.tile([P, CH, NJ], F32)
         x = norm.tile([P, NJ, CH], F32)
+        last_acc = []
 
         for r in range(ROUNDS):
             mask_a = mask_pool.tile([P, ROUND * K_PASS], BF16)
@@ -180,44 +181,61 @@ def tile_trianglemultiplicativeupdate_pa_k_kernel(
                         out=x_sum[:, ch, :], in0=acc[:], in1=x_sum[:, ch, :], op=ALU.add
                     )
                 else:
-                    nc.vector.tensor_tensor(
-                        out=x[:, :, ch],
-                        in0=acc[:].rearrange("p d j -> p j d"),
-                        in1=x_sum[:, ch, :].rearrange("p d j -> p j d"),
-                        op=ALU.add,
-                    )
+                    last_acc.append(acc)
 
         total = norm.tile([P, NJ], F32)
-        nc.vector.tensor_reduce(out=total[:], in_=x[:], axis=mybir.AxisListType.X, op=ALU.add)
         centred = norm.tile([P, NJ, CH], F32)
-        nc.vector.scalar_tensor_tensor(
-            out=centred[:],
-            in0=total[:].unsqueeze(2).to_broadcast([P, NJ, CH]),
-            scalar=-1.0 / CH,
-            in1=x[:],
-            op0=ALU.mult,
-            op1=ALU.add,
-        )
         squares = norm.tile([P, NJ, CH], F32)
-        nc.scalar.activation(out=squares[:], in_=centred[:], func=ACT.Square)
         weighted = norm.tile([P, NJ, CH], F32)
-        nc.gpsimd.tensor_tensor(
-            out=weighted[:],
-            in0=centred[:],
-            in1=gain[:].unsqueeze(1).to_broadcast([P, NJ, CH]),
-            op=ALU.mult,
-        )
         spread = norm.tile([P, NJ], F32)
-        nc.vector.tensor_reduce(out=spread[:], in_=squares[:], axis=mybir.AxisListType.X, op=ALU.add)
         std = norm.tile([P, NJ], F32)
-        nc.scalar.activation(out=std[:], in_=spread[:], func=ACT.Sqrt, bias=eps_col[:], scale=1.0 / CH)
         rstd = norm.tile([P, NJ], F32)
-        nc.vector.reciprocal(out=rstd[:], in_=std[:])
         y = norm.tile([P, NJ, CH], F32)
-        nc.vector.tensor_tensor(
-            out=y[:], in0=weighted[:], in1=rstd[:].unsqueeze(2).to_broadcast([P, NJ, CH]), op=ALU.mult
-        )
-        nc.vector.tensor_tensor(
-            out=y[:], in0=y[:], in1=bias[:].unsqueeze(1).to_broadcast([P, NJ, CH]), op=ALU.add
-        )
-        nc.sync.dma_start(out=out[0].rearrange("i j d -> i (j d)"), in_=y[:].rearrange("p j d -> p (j d)"))
+        J_HALF = NJ // 2
+        for js in (slice(0, J_HALF), slice(J_HALF, NJ)):
+            for h in range(CH // HALF):
+                ch = slice(h * HALF, (h + 1) * HALF)
+                nc.vector.tensor_tensor(
+                    out=x[:, js, ch],
+                    in0=last_acc[h][:, :, js].rearrange("p d j -> p j d"),
+                    in1=x_sum[:, ch, js].rearrange("p d j -> p j d"),
+                    op=ALU.add,
+                )
+            nc.vector.tensor_reduce(
+                out=total[:, js], in_=x[:, js, :], axis=mybir.AxisListType.X, op=ALU.add
+            )
+            nc.vector.scalar_tensor_tensor(
+                out=centred[:, js, :],
+                in0=total[:, js].unsqueeze(2).to_broadcast([P, J_HALF, CH]),
+                scalar=-1.0 / CH,
+                in1=x[:, js, :],
+                op0=ALU.mult,
+                op1=ALU.add,
+            )
+            nc.scalar.activation(out=squares[:, js, :], in_=centred[:, js, :], func=ACT.Square)
+            nc.gpsimd.tensor_tensor(
+                out=weighted[:, js, :],
+                in0=centred[:, js, :],
+                in1=gain[:].unsqueeze(1).to_broadcast([P, J_HALF, CH]),
+                op=ALU.mult,
+            )
+            nc.vector.tensor_reduce(
+                out=spread[:, js], in_=squares[:, js, :], axis=mybir.AxisListType.X, op=ALU.add
+            )
+            nc.scalar.activation(
+                out=std[:, js], in_=spread[:, js], func=ACT.Sqrt, bias=eps_col[:], scale=1.0 / CH
+            )
+            nc.vector.reciprocal(out=rstd[:, js], in_=std[:, js])
+            nc.vector.tensor_tensor(
+                out=y[:, js, :],
+                in0=weighted[:, js, :],
+                in1=rstd[:, js].unsqueeze(2).to_broadcast([P, J_HALF, CH]),
+                op=ALU.mult,
+            )
+            nc.vector.tensor_tensor(
+                out=y[:, js, :],
+                in0=y[:, js, :],
+                in1=bias[:].unsqueeze(1).to_broadcast([P, J_HALF, CH]),
+                op=ALU.add,
+            )
+            nc.sync.dma_start(out=out[0][:, js, :], in_=y[:, js, :])

@@ -5,7 +5,6 @@ from concourse.masks import make_identity
 
 F32 = mybir.dt.float32
 BF16 = mybir.dt.bfloat16
-I32 = mybir.dt.int32
 U32 = mybir.dt.uint32
 U8 = mybir.dt.uint8
 FP8X4 = mybir.dt.float8_e4m3fn_x4
@@ -24,7 +23,8 @@ ROUND = 4
 ROUNDS = PASSES // ROUND
 PAIRS = CH // 2
 HALF = CH // 2
-J_SCALAR = 64
+J_SCALAR = 40
+J_HALF = NJ // 2
 EPS = 1e-5
 
 FLOPS = 2 * NI * NJ * NK * CH
@@ -35,19 +35,20 @@ def tile_trianglemultiplicativeupdate_pa_k_kernel(
 ):
     nc = tc.nc
     a_rows = a_gated[0].rearrange("i (g k) d -> g i (k d)", k=K_PASS)
-    b_rows = b_gated[0].rearrange("(g t p) j d -> g p t (j d)", t=PACK, p=P)
+    b_rows = b_gated[0].rearrange("(g u q e) j d -> g q u (e j d)", u=2, q=P, e=2)
     mask_a_rows = mask_ik[0].rearrange("i (r k) -> r i k", r=ROUNDS)
-    mask_b_rows = mask_kj[0].rearrange("(r c p) j -> r p c j", r=ROUNDS, p=P)
+    mask_b_rows = mask_kj[0].rearrange("(r n p) j -> r p n j", r=ROUNDS, p=P)
 
     with ExitStack() as ctx:
         const = ctx.enter_context(tc.tile_pool(name="const", bufs=1))
         mask_pool = ctx.enter_context(tc.tile_pool(name="mask_pool", bufs=2))
-        keeps = ctx.enter_context(tc.tile_pool(name="keeps", bufs=1))
         loads = ctx.enter_context(tc.tile_pool(name="loads", bufs=3))
         grouped = ctx.enter_context(tc.tile_pool(name="grouped", bufs=2))
         quant = ctx.enter_context(tc.tile_pool(name="quant", bufs=2))
         norm = ctx.enter_context(tc.tile_pool(name="norm", bufs=1))
-        turn_psum = ctx.enter_context(tc.psum_pool(name="turn_psum", bufs=6))
+        turn_psum = ctx.enter_context(tc.psum_pool(name="turn_psum", bufs=3))
+        mask_turn_psum = ctx.enter_context(tc.psum_pool(name="mask_turn_psum", bufs=1))
+        mask_psum = ctx.enter_context(tc.psum_pool(name="mask_psum", bufs=2))
         acc_psum = ctx.enter_context(tc.psum_pool(name="acc_psum", bufs=1))
 
         eps_col = const.tile([P, 1], F32)
@@ -56,6 +57,8 @@ def tile_trianglemultiplicativeupdate_pa_k_kernel(
         nc.scalar.activation(out=warm[:], in_=eps_col[:], func=ACT.Sqrt)
         ident = const.tile([P, P], F32)
         make_identity(nc, ident[:])
+        ident_bf = const.tile([P, P], BF16)
+        make_identity(nc, ident_bf[:])
         gain_bf = const.tile([P, CH], BF16)
         nc.gpsimd.dma_start(out=gain_bf[:], in_=ln_out_w.partition_broadcast(P))
         bias_bf = const.tile([P, CH], BF16)
@@ -72,16 +75,9 @@ def tile_trianglemultiplicativeupdate_pa_k_kernel(
         for r in range(ROUNDS):
             mask_a = mask_pool.tile([P, ROUND * K_PASS], BF16)
             nc.sync.dma_start(out=mask_a[:], in_=mask_a_rows[r])
+            mask_a_words = mask_a[:].bitcast(F32).rearrange("p (c u q) -> p c u q", c=ROUND, u=2)
             mask_b = mask_pool.tile([P, ROUND * PACK, NJ], BF16)
             nc.sync.dma_start(out=mask_b[:], in_=mask_b_rows[r])
-            keep_a = keeps.tile([P, ROUND * K_PASS], I32)
-            nc.vector.tensor_scalar(
-                out=keep_a[:], in0=mask_a[:], scalar1=-1.0, scalar2=None, op0=ALU.mult
-            )
-            keep_b = keeps.tile([P, ROUND * PACK, J_SCALAR], I32)
-            nc.vector.tensor_scalar(
-                out=keep_b[:], in0=mask_b[:, :, :J_SCALAR], scalar1=-1.0, scalar2=None, op0=ALU.mult
-            )
 
             a_codes = quant.tile([P, ROUND, CH * NI], U32, align_bytes=64)
             a_scales = quant.tile([P, ROUND, CH * NI], U8, align_bytes=64)
@@ -93,80 +89,93 @@ def tile_trianglemultiplicativeupdate_pa_k_kernel(
                 a_nat = loads.tile([P, K_PASS * CH], BF16)
                 nc.sync.dma_start(out=a_nat[:], in_=a_rows[g])
                 b_nat = loads.tile([P, PACK, NJ, CH], BF16)
-                nc.sync.dma_start(out=b_nat[:].rearrange("p t j d -> p t (j d)"), in_=b_rows[g])
-
-                a_words = a_nat[:].bitcast(I32).rearrange("p (k u) -> p k u", u=PAIRS)
-                nc.vector.tensor_tensor(
-                    out=a_words,
-                    in0=a_words,
-                    in1=keep_a[:, c * K_PASS : (c + 1) * K_PASS]
-                    .unsqueeze(2)
-                    .to_broadcast([P, K_PASS, PAIRS]),
-                    op=ALU.bitwise_and,
+                nc.sync.dma_start(
+                    out=b_nat[:].rearrange("p (u e) j d -> p u (e j d)", u=2), in_=b_rows[g]
                 )
-                a_f32 = a_nat[:].bitcast(F32).rearrange("p (t k u) -> p t k u", t=PACK, u=PAIRS)
-                a_grouped = grouped.tile([P, CH, NI, PACK], BF16, align_bytes=64)
-                for u in range(PAIRS):
+
+                mask_words = mask_psum.tile([P, 2, P, 2], F32)
+                for u in range(2):
+                    nc.tensor.transpose(mask_words[:, 0, :, u], mask_a_words[:, c, u, :], ident[:])
+                mask_b_turned = mask_turn_psum.tile([P, PACK, P], BF16)
+                for n in range(PACK):
+                    nc.tensor.transpose(
+                        mask_b_turned[:, n, :], mask_b[:, c * PACK + n, :], ident_bf[:]
+                    )
+                mask_b_rows_j = mask_pool.tile([P, K_PASS], BF16)
+                nc.scalar.copy(
+                    out=mask_b_rows_j[:], in_=mask_b_turned[:].rearrange("p n k -> p (n k)")
+                )
+                for u in range(2):
+                    nc.tensor.transpose(
+                        mask_words[:, 1, :, u],
+                        mask_b_rows_j[:].bitcast(F32)[:, u * P : (u + 1) * P],
+                        ident[:],
+                    )
+                mask_values = mask_words[:].rearrange("p w n u -> p (w n u)").bitcast(BF16)
+
+                a_f32 = a_nat[:].bitcast(F32).rearrange(
+                    "p (u q e w) -> p u e q w", u=2, e=2, w=PAIRS
+                )
+                a_grouped = grouped.tile([P, CH, NI * PACK], BF16, align_bytes=64)
+                for w in range(PAIRS):
                     turned = turn_psum.tile([P, PACK * NI], F32)
                     for t in range(PACK):
                         nc.tensor.transpose(
-                            turned[:, t * NI : (t + 1) * NI], a_f32[:, t, :, u], ident[:]
+                            turned[:, t * NI : (t + 1) * NI], a_f32[:, t // 2, t % 2, :, w], ident[:]
                         )
                     nc.scalar.copy(
-                        out=a_grouped[:, 2 * u : 2 * u + 2, :, :],
-                        in_=turned[:].bitcast(BF16).rearrange("p (t i e) -> p e i t", t=PACK, e=2),
+                        out=a_grouped[:, 2 * w : 2 * w + 2, :].rearrange(
+                            "p s (i t) -> p s i t", t=PACK
+                        ),
+                        in_=turned[:].bitcast(BF16).rearrange("p (t i s) -> p s i t", t=PACK, s=2),
                     )
 
-                b_words = (
-                    b_nat[:]
-                    .rearrange("p t j d -> p (t j d)")
-                    .bitcast(I32)
-                    .rearrange("p (t j u) -> p t j u", t=PACK, u=PAIRS)
-                )
-                nc.vector.tensor_tensor(
-                    out=b_words[:, :, :J_SCALAR, :],
-                    in0=b_words[:, :, :J_SCALAR, :],
-                    in1=keep_b[:, c * PACK : (c + 1) * PACK, :]
-                    .unsqueeze(3)
-                    .to_broadcast([P, PACK, J_SCALAR, PAIRS]),
-                    op=ALU.bitwise_and,
-                )
-                b_grouped = grouped.tile([P, CH, NJ, PACK], BF16, align_bytes=64)
+                b_grouped = grouped.tile([P, CH, NJ * PACK], BF16, align_bytes=64)
+                b_target = b_grouped[:].rearrange("p d (j t) -> p j d t", t=PACK)
+                b_source = b_nat[:].rearrange("p t j d -> p j d t")
                 for h in range(CH // HALF):
                     ch = slice(h * HALF, (h + 1) * HALF)
-                    nc.scalar.copy(
-                        out=b_grouped[:, ch, :J_SCALAR, :].rearrange("p d j t -> p j d t"),
-                        in_=b_nat[:, :, :J_SCALAR, ch].rearrange("p t j d -> p j d t"),
-                    )
-                    nc.vector.tensor_tensor(
-                        out=b_grouped[:, ch, J_SCALAR:, :].rearrange("p d j t -> p j d t"),
-                        in0=b_nat[:, :, J_SCALAR:, ch].rearrange("p t j d -> p j d t"),
-                        in1=mask_b[:, c * PACK : (c + 1) * PACK, J_SCALAR:]
-                        .rearrange("p t j -> p j t")
-                        .unsqueeze(2)
-                        .to_broadcast([P, NJ - J_SCALAR, HALF, PACK]),
-                        op=ALU.mult,
+                    nc.scalar.copy(out=b_target[:, :J_SCALAR, ch, :], in_=b_source[:, :J_SCALAR, ch, :])
+                    nc.gpsimd.tensor_scalar(
+                        out=b_target[:, J_SCALAR:, ch, :],
+                        in0=b_source[:, J_SCALAR:, ch, :],
+                        scalar1=1.0,
+                        scalar2=0.0,
+                        op0=ALU.mult,
+                        op1=ALU.add,
                     )
 
-                nc.vector.quantize_mx(
-                    out=b_codes[:, c, :].bitcast(FP8X4),
-                    scales=b_scales[:, c, :],
-                    in_=b_grouped[:].rearrange("p d j t -> p (d j t)"),
+                nc.vector.tensor_tensor(
+                    out=a_grouped[:],
+                    in0=a_grouped[:],
+                    in1=mask_values[:, : NI * PACK].unsqueeze(1).to_broadcast([P, CH, NI * PACK]),
+                    op=ALU.mult,
+                )
+                nc.vector.tensor_tensor(
+                    out=b_grouped[:],
+                    in0=b_grouped[:],
+                    in1=mask_values[:, NI * PACK :].unsqueeze(1).to_broadcast([P, CH, NJ * PACK]),
+                    op=ALU.mult,
                 )
                 nc.vector.quantize_mx(
                     out=a_codes[:, c, :].bitcast(FP8X4),
                     scales=a_scales[:, c, :],
-                    in_=a_grouped[:].rearrange("p d i t -> p (d i t)"),
+                    in_=a_grouped[:].rearrange("p d n -> p (d n)"),
+                )
+                nc.vector.quantize_mx(
+                    out=b_codes[:, c, :].bitcast(FP8X4),
+                    scales=b_scales[:, c, :],
+                    in_=b_grouped[:].rearrange("p d n -> p (d n)"),
                 )
 
             for h in range(CH // HALF):
                 ch = slice(h * HALF, (h + 1) * HALF)
                 acc = acc_psum.tile([P, HALF, NJ], F32, tag="acc%d" % h)
-                for q in range(HALF):
-                    cols = slice((h * HALF + q) * P, (h * HALF + q + 1) * P)
+                for s in range(HALF):
+                    cols = slice((h * HALF + s) * P, (h * HALF + s + 1) * P)
                     for c in range(ROUND):
                         nc.tensor.matmul_mx(
-                            out=acc[:, q, :],
+                            out=acc[:, s, :],
                             lhsT=a_codes[:, c, cols].bitcast(FP8X4),
                             lhsT_scale=a_scales[:, c, cols],
                             rhs=b_codes[:, c, cols].bitcast(FP8X4),
@@ -191,7 +200,6 @@ def tile_trianglemultiplicativeupdate_pa_k_kernel(
         std = norm.tile([P, NJ], F32)
         rstd = norm.tile([P, NJ], F32)
         y = norm.tile([P, NJ, CH], F32)
-        J_HALF = NJ // 2
         for js in (slice(0, J_HALF), slice(J_HALF, NJ)):
             for h in range(CH // HALF):
                 ch = slice(h * HALF, (h + 1) * HALF)

@@ -25,6 +25,7 @@ PAIRS = CH // 2
 HALF = CH // 2
 J_SCALAR = 40
 J_HALF = NJ // 2
+LAG = 2
 EPS = 1e-5
 
 FLOPS = 2 * NI * NJ * NK * CH
@@ -36,12 +37,12 @@ def tile_trianglemultiplicativeupdate_pa_k_kernel(
     nc = tc.nc
     a_rows = a_gated[0].rearrange("i (g k) d -> g i (k d)", k=K_PASS)
     b_rows = b_gated[0].rearrange("(g u q e) j d -> g q u (e j d)", u=2, q=P, e=2)
-    mask_a_rows = mask_ik[0].rearrange("i (r k) -> r i k", r=ROUNDS)
-    mask_b_rows = mask_kj[0].rearrange("(r n p) j -> r p n j", r=ROUNDS, p=P)
+    mask_a_rows = mask_ik[0].rearrange("i (g k) -> g i k", k=K_PASS)
+    mask_b_rows = mask_kj[0].rearrange("(g n p) j -> g p n j", n=PACK, p=P)
 
     with ExitStack() as ctx:
         const = ctx.enter_context(tc.tile_pool(name="const", bufs=1))
-        mask_pool = ctx.enter_context(tc.tile_pool(name="mask_pool", bufs=2))
+        mask_pool = ctx.enter_context(tc.tile_pool(name="mask_pool", bufs=3))
         loads = ctx.enter_context(tc.tile_pool(name="loads", bufs=3))
         grouped = ctx.enter_context(tc.tile_pool(name="grouped", bufs=2))
         quant = ctx.enter_context(tc.tile_pool(name="quant", bufs=2))
@@ -51,123 +52,118 @@ def tile_trianglemultiplicativeupdate_pa_k_kernel(
         mask_psum = ctx.enter_context(tc.psum_pool(name="mask_psum", bufs=2))
         acc_psum = ctx.enter_context(tc.psum_pool(name="acc_psum", bufs=1))
 
-        eps_col = const.tile([P, 1], F32)
-        nc.vector.memset(eps_col[:], EPS)
-        warm = const.tile([P, 1], F32)
-        nc.scalar.activation(out=warm[:], in_=eps_col[:], func=ACT.Sqrt)
         ident = const.tile([P, P], F32)
         make_identity(nc, ident[:])
         ident_bf = const.tile([P, P], BF16)
         make_identity(nc, ident_bf[:])
+        eps_col = const.tile([P, 1], F32)
+        nc.vector.memset(eps_col[:], EPS)
+        warm = const.tile([P, 1], F32)
+        nc.scalar.activation(out=warm[:], in_=eps_col[:], func=ACT.Sqrt)
         gain_bf = const.tile([P, CH], BF16)
-        nc.gpsimd.dma_start(out=gain_bf[:], in_=ln_out_w.partition_broadcast(P))
+        nc.scalar.dma_start(out=gain_bf[:], in_=ln_out_w.partition_broadcast(P))
         bias_bf = const.tile([P, CH], BF16)
-        nc.gpsimd.dma_start(out=bias_bf[:], in_=ln_out_b.partition_broadcast(P))
+        nc.scalar.dma_start(out=bias_bf[:], in_=ln_out_b.partition_broadcast(P))
         gain = const.tile([P, CH], F32)
         nc.gpsimd.tensor_copy(out=gain[:], in_=gain_bf[:])
         bias = const.tile([P, CH], F32)
         nc.gpsimd.tensor_copy(out=bias[:], in_=bias_bf[:])
 
         x_sum = const.tile([P, CH, NJ], F32)
-        x = norm.tile([P, NJ, CH], F32)
+        codes = {}
         last_acc = []
 
-        for r in range(ROUNDS):
-            mask_a = mask_pool.tile([P, ROUND * K_PASS], BF16)
-            nc.sync.dma_start(out=mask_a[:], in_=mask_a_rows[r])
-            mask_a_words = mask_a[:].bitcast(F32).rearrange("p (c u q) -> p c u q", c=ROUND, u=2)
-            mask_b = mask_pool.tile([P, ROUND * PACK, NJ], BF16)
-            nc.sync.dma_start(out=mask_b[:], in_=mask_b_rows[r])
+        def prepare_and_quantise(g):
+            r, c = divmod(g, ROUND)
+            if c == 0:
+                a_codes = quant.tile([P, ROUND, CH * NI], U32, align_bytes=64)
+                a_scales = quant.tile([P, ROUND, CH * NI], U8, align_bytes=64)
+                b_codes = quant.tile([P, ROUND, CH * NJ], U32, align_bytes=64)
+                b_scales = quant.tile([P, ROUND, CH * NJ], U8, align_bytes=64)
+                codes[r] = (a_codes, a_scales, b_codes, b_scales)
+            a_codes, a_scales, b_codes, b_scales = codes[r]
 
-            a_codes = quant.tile([P, ROUND, CH * NI], U32, align_bytes=64)
-            a_scales = quant.tile([P, ROUND, CH * NI], U8, align_bytes=64)
-            b_codes = quant.tile([P, ROUND, CH * NJ], U32, align_bytes=64)
-            b_scales = quant.tile([P, ROUND, CH * NJ], U8, align_bytes=64)
+            mask_b = mask_pool.tile([P, PACK, NJ], BF16)
+            nc.sync.dma_start(out=mask_b[:], in_=mask_b_rows[g])
+            mask_a = mask_pool.tile([P, K_PASS], BF16)
+            nc.sync.dma_start(out=mask_a[:], in_=mask_a_rows[g])
+            a_nat = loads.tile([P, K_PASS * CH], BF16)
+            nc.sync.dma_start(out=a_nat[:], in_=a_rows[g])
+            b_nat = loads.tile([P, PACK, NJ, CH], BF16)
+            nc.sync.dma_start(
+                out=b_nat[:].rearrange("p (u e) j d -> p u (e j d)", u=2), in_=b_rows[g]
+            )
 
-            for c in range(ROUND):
-                g = r * ROUND + c
-                a_nat = loads.tile([P, K_PASS * CH], BF16)
-                nc.sync.dma_start(out=a_nat[:], in_=a_rows[g])
-                b_nat = loads.tile([P, PACK, NJ, CH], BF16)
-                nc.sync.dma_start(
-                    out=b_nat[:].rearrange("p (u e) j d -> p u (e j d)", u=2), in_=b_rows[g]
-                )
+            mask_b_turned = mask_turn_psum.tile([P, PACK, P], BF16)
+            for n in range(PACK):
+                nc.tensor.transpose(mask_b_turned[:, n, :], mask_b[:, n, :], ident_bf[:])
+            mask_b_rows_j = mask_pool.tile([P, K_PASS], BF16)
+            nc.scalar.copy(out=mask_b_rows_j[:], in_=mask_b_turned[:].rearrange("p n k -> p (n k)"))
 
-                mask_words = mask_psum.tile([P, 2, P, 2], F32)
-                for u in range(2):
-                    nc.tensor.transpose(mask_words[:, 0, :, u], mask_a_words[:, c, u, :], ident[:])
-                mask_b_turned = mask_turn_psum.tile([P, PACK, P], BF16)
-                for n in range(PACK):
+            a_f32 = a_nat[:].bitcast(F32).rearrange("p (u q e w) -> p u e q w", u=2, e=2, w=PAIRS)
+            a_grouped = grouped.tile([P, CH, NI * PACK], BF16, align_bytes=64)
+            for w in range(PAIRS):
+                turned = turn_psum.tile([P, PACK * NI], F32)
+                for t in range(PACK):
                     nc.tensor.transpose(
-                        mask_b_turned[:, n, :], mask_b[:, c * PACK + n, :], ident_bf[:]
+                        turned[:, t * NI : (t + 1) * NI], a_f32[:, t // 2, t % 2, :, w], ident[:]
                     )
-                mask_b_rows_j = mask_pool.tile([P, K_PASS], BF16)
-                nc.scalar.copy(
-                    out=mask_b_rows_j[:], in_=mask_b_turned[:].rearrange("p n k -> p (n k)")
-                )
-                for u in range(2):
-                    nc.tensor.transpose(
-                        mask_words[:, 1, :, u],
-                        mask_b_rows_j[:].bitcast(F32)[:, u * P : (u + 1) * P],
-                        ident[:],
-                    )
-                mask_values = mask_words[:].rearrange("p w n u -> p (w n u)").bitcast(BF16)
+                target = a_grouped[:, 2 * w : 2 * w + 2, :].rearrange("p s (i t) -> p s i t", t=PACK)
+                source = turned[:].bitcast(BF16).rearrange("p (t i s) -> p s i t", t=PACK, s=2)
+                if g == 0 and w % 2 == 1:
+                    nc.vector.tensor_copy(out=target, in_=source)
+                else:
+                    nc.scalar.copy(out=target, in_=source)
 
-                a_f32 = a_nat[:].bitcast(F32).rearrange(
-                    "p (u q e w) -> p u e q w", u=2, e=2, w=PAIRS
+            mask_words = mask_psum.tile([P, 2, P, 2], F32)
+            for u in range(2):
+                half = slice(u * P, (u + 1) * P)
+                nc.tensor.transpose(mask_words[:, 0, :, u], mask_a[:].bitcast(F32)[:, half], ident[:])
+                nc.tensor.transpose(
+                    mask_words[:, 1, :, u], mask_b_rows_j[:].bitcast(F32)[:, half], ident[:]
                 )
-                a_grouped = grouped.tile([P, CH, NI * PACK], BF16, align_bytes=64)
-                for w in range(PAIRS):
-                    turned = turn_psum.tile([P, PACK * NI], F32)
-                    for t in range(PACK):
-                        nc.tensor.transpose(
-                            turned[:, t * NI : (t + 1) * NI], a_f32[:, t // 2, t % 2, :, w], ident[:]
-                        )
-                    nc.scalar.copy(
-                        out=a_grouped[:, 2 * w : 2 * w + 2, :].rearrange(
-                            "p s (i t) -> p s i t", t=PACK
-                        ),
-                        in_=turned[:].bitcast(BF16).rearrange("p (t i s) -> p s i t", t=PACK, s=2),
-                    )
+            mask_values = mask_words[:].rearrange("p w n u -> p (w n u)").bitcast(BF16)
 
-                b_grouped = grouped.tile([P, CH, NJ * PACK], BF16, align_bytes=64)
-                b_target = b_grouped[:].rearrange("p d (j t) -> p j d t", t=PACK)
-                b_source = b_nat[:].rearrange("p t j d -> p j d t")
-                for h in range(CH // HALF):
-                    ch = slice(h * HALF, (h + 1) * HALF)
-                    nc.scalar.copy(out=b_target[:, :J_SCALAR, ch, :], in_=b_source[:, :J_SCALAR, ch, :])
-                    nc.gpsimd.tensor_scalar(
-                        out=b_target[:, J_SCALAR:, ch, :],
-                        in0=b_source[:, J_SCALAR:, ch, :],
-                        scalar1=1.0,
-                        scalar2=0.0,
-                        op0=ALU.mult,
-                        op1=ALU.add,
-                    )
-
-                nc.vector.tensor_tensor(
-                    out=a_grouped[:],
-                    in0=a_grouped[:],
-                    in1=mask_values[:, : NI * PACK].unsqueeze(1).to_broadcast([P, CH, NI * PACK]),
-                    op=ALU.mult,
-                )
-                nc.vector.tensor_tensor(
-                    out=b_grouped[:],
-                    in0=b_grouped[:],
-                    in1=mask_values[:, NI * PACK :].unsqueeze(1).to_broadcast([P, CH, NJ * PACK]),
-                    op=ALU.mult,
-                )
-                nc.vector.quantize_mx(
-                    out=a_codes[:, c, :].bitcast(FP8X4),
-                    scales=a_scales[:, c, :],
-                    in_=a_grouped[:].rearrange("p d n -> p (d n)"),
-                )
-                nc.vector.quantize_mx(
-                    out=b_codes[:, c, :].bitcast(FP8X4),
-                    scales=b_scales[:, c, :],
-                    in_=b_grouped[:].rearrange("p d n -> p (d n)"),
+            b_grouped = grouped.tile([P, CH, NJ * PACK], BF16, align_bytes=64)
+            b_target = b_grouped[:].rearrange("p d (j t) -> p j d t", t=PACK)
+            b_source = b_nat[:].rearrange("p t j d -> p j d t")
+            for h in range(CH // HALF):
+                ch = slice(h * HALF, (h + 1) * HALF)
+                nc.scalar.copy(out=b_target[:, :J_SCALAR, ch, :], in_=b_source[:, :J_SCALAR, ch, :])
+                nc.gpsimd.tensor_scalar(
+                    out=b_target[:, J_SCALAR:, ch, :],
+                    in0=b_source[:, J_SCALAR:, ch, :],
+                    scalar1=1.0,
+                    scalar2=0.0,
+                    op0=ALU.mult,
+                    op1=ALU.add,
                 )
 
+            nc.vector.tensor_tensor(
+                out=a_grouped[:],
+                in0=a_grouped[:],
+                in1=mask_values[:, : NI * PACK].unsqueeze(1).to_broadcast([P, CH, NI * PACK]),
+                op=ALU.mult,
+            )
+            nc.vector.tensor_tensor(
+                out=b_grouped[:],
+                in0=b_grouped[:],
+                in1=mask_values[:, NI * PACK :].unsqueeze(1).to_broadcast([P, CH, NJ * PACK]),
+                op=ALU.mult,
+            )
+            nc.vector.quantize_mx(
+                out=a_codes[:, c, :].bitcast(FP8X4),
+                scales=a_scales[:, c, :],
+                in_=a_grouped[:].rearrange("p d n -> p (d n)"),
+            )
+            nc.vector.quantize_mx(
+                out=b_codes[:, c, :].bitcast(FP8X4),
+                scales=b_scales[:, c, :],
+                in_=b_grouped[:].rearrange("p d n -> p (d n)"),
+            )
+
+        def multiply(r):
+            a_codes, a_scales, b_codes, b_scales = codes[r]
             for h in range(CH // HALF):
                 ch = slice(h * HALF, (h + 1) * HALF)
                 acc = acc_psum.tile([P, HALF, NJ], F32, tag="acc%d" % h)
@@ -192,6 +188,13 @@ def tile_trianglemultiplicativeupdate_pa_k_kernel(
                 else:
                     last_acc.append(acc)
 
+        for g in range(PASSES):
+            prepare_and_quantise(g)
+            if g >= ROUND + LAG - 1 and (g - LAG + 1) % ROUND == 0:
+                multiply((g - LAG + 1) // ROUND - 1)
+        multiply(ROUNDS - 1)
+
+        x = norm.tile([P, NJ, CH], F32)
         total = norm.tile([P, NJ], F32)
         centred = norm.tile([P, NJ, CH], F32)
         squares = norm.tile([P, NJ, CH], F32)

@@ -19,13 +19,11 @@ CH = 8
 PACK = 4
 K_PASS = P * PACK
 PASSES = NK // K_PASS
-ROUND = 4
-ROUNDS = PASSES // ROUND
+ROUNDS = (6, 5, 4, 1)
 PAIRS = CH // 2
 HALF = CH // 2
 J_SCALAR = 40
 J_HALF = NJ // 2
-LAG = 2
 EPS = 1e-5
 
 FLOPS = 2 * NI * NJ * NK * CH
@@ -45,7 +43,7 @@ def tile_trianglemultiplicativeupdate_pa_k_kernel(
         mask_pool = ctx.enter_context(tc.tile_pool(name="mask_pool", bufs=3))
         loads = ctx.enter_context(tc.tile_pool(name="loads", bufs=3))
         grouped = ctx.enter_context(tc.tile_pool(name="grouped", bufs=2))
-        quant = ctx.enter_context(tc.tile_pool(name="quant", bufs=2))
+        quant = ctx.enter_context(tc.tile_pool(name="quant", bufs=11))
         norm = ctx.enter_context(tc.tile_pool(name="norm", bufs=1))
         turn_psum = ctx.enter_context(tc.psum_pool(name="turn_psum", bufs=3))
         mask_turn_psum = ctx.enter_context(tc.psum_pool(name="mask_turn_psum", bufs=1))
@@ -61,60 +59,58 @@ def tile_trianglemultiplicativeupdate_pa_k_kernel(
         warm = const.tile([P, 1], F32)
         nc.scalar.activation(out=warm[:], in_=eps_col[:], func=ACT.Sqrt)
         gain_bf = const.tile([P, CH], BF16)
-        nc.scalar.dma_start(out=gain_bf[:], in_=ln_out_w.partition_broadcast(P))
         bias_bf = const.tile([P, CH], BF16)
-        nc.scalar.dma_start(out=bias_bf[:], in_=ln_out_b.partition_broadcast(P))
         gain = const.tile([P, CH], F32)
-        nc.gpsimd.tensor_copy(out=gain[:], in_=gain_bf[:])
         bias = const.tile([P, CH], F32)
-        nc.gpsimd.tensor_copy(out=bias[:], in_=bias_bf[:])
 
         x_sum = const.tile([P, CH, NJ], F32)
-        codes = {}
-        last_acc = []
+        state = {}
 
-        def prepare_and_quantise(g):
-            r, c = divmod(g, ROUND)
-            if c == 0:
-                a_codes = quant.tile([P, ROUND, CH * NI], U32, align_bytes=64)
-                a_scales = quant.tile([P, ROUND, CH * NI], U8, align_bytes=64)
-                b_codes = quant.tile([P, ROUND, CH * NJ], U32, align_bytes=64)
-                b_scales = quant.tile([P, ROUND, CH * NJ], U8, align_bytes=64)
-                codes[r] = (a_codes, a_scales, b_codes, b_scales)
-            a_codes, a_scales, b_codes, b_scales = codes[r]
-
+        def load(g):
+            a_nat = loads.tile([P, K_PASS * CH], BF16)
+            nc.sync.dma_start(out=a_nat[:], in_=a_rows[g])
             mask_b = mask_pool.tile([P, PACK, NJ], BF16)
             nc.sync.dma_start(out=mask_b[:], in_=mask_b_rows[g])
             mask_a = mask_pool.tile([P, K_PASS], BF16)
             nc.sync.dma_start(out=mask_a[:], in_=mask_a_rows[g])
-            a_nat = loads.tile([P, K_PASS * CH], BF16)
-            nc.sync.dma_start(out=a_nat[:], in_=a_rows[g])
             b_nat = loads.tile([P, PACK, NJ, CH], BF16)
             nc.sync.dma_start(
                 out=b_nat[:].rearrange("p (u e) j d -> p u (e j d)", u=2), in_=b_rows[g]
             )
+            state["loads", g] = (mask_a, mask_b, a_nat, b_nat)
 
+        def turn_mask_b(g):
+            mask_b = state["loads", g][1]
             mask_b_turned = mask_turn_psum.tile([P, PACK, P], BF16)
             for n in range(PACK):
                 nc.tensor.transpose(mask_b_turned[:, n, :], mask_b[:, n, :], ident_bf[:])
             mask_b_rows_j = mask_pool.tile([P, K_PASS], BF16)
             nc.scalar.copy(out=mask_b_rows_j[:], in_=mask_b_turned[:].rearrange("p n k -> p (n k)"))
+            state["mask_b_rows_j", g] = mask_b_rows_j
 
+        def turn_a(g, pairs):
+            a_nat = state["loads", g][2]
             a_f32 = a_nat[:].bitcast(F32).rearrange("p (u q e w) -> p u e q w", u=2, e=2, w=PAIRS)
-            a_grouped = grouped.tile([P, CH, NI * PACK], BF16, align_bytes=64)
-            for w in range(PAIRS):
+            if pairs[0] == 0:
+                state["a_grouped", g] = grouped.tile(
+                    [P, CH, NI * PACK], BF16, name="a_grouped", align_bytes=64
+                )
+            a_grouped = state["a_grouped", g]
+            for w in pairs:
                 turned = turn_psum.tile([P, PACK * NI], F32)
                 for t in range(PACK):
                     nc.tensor.transpose(
                         turned[:, t * NI : (t + 1) * NI], a_f32[:, t // 2, t % 2, :, w], ident[:]
                     )
-                target = a_grouped[:, 2 * w : 2 * w + 2, :].rearrange("p s (i t) -> p s i t", t=PACK)
-                source = turned[:].bitcast(BF16).rearrange("p (t i s) -> p s i t", t=PACK, s=2)
-                if g == 0 and w % 2 == 1:
-                    nc.vector.tensor_copy(out=target, in_=source)
-                else:
-                    nc.scalar.copy(out=target, in_=source)
+                copy = nc.vector.tensor_copy if g == 0 and w % 2 == 1 else nc.scalar.copy
+                copy(
+                    out=a_grouped[:, 2 * w : 2 * w + 2, :].rearrange("p s (i t) -> p s i t", t=PACK),
+                    in_=turned[:].bitcast(BF16).rearrange("p (t i s) -> p s i t", t=PACK, s=2),
+                )
 
+        def turn_mask_words(g):
+            mask_a = state["loads", g][0]
+            mask_b_rows_j = state["mask_b_rows_j", g]
             mask_words = mask_psum.tile([P, 2, P, 2], F32)
             for u in range(2):
                 half = slice(u * P, (u + 1) * P)
@@ -122,8 +118,10 @@ def tile_trianglemultiplicativeupdate_pa_k_kernel(
                 nc.tensor.transpose(
                     mask_words[:, 1, :, u], mask_b_rows_j[:].bitcast(F32)[:, half], ident[:]
                 )
-            mask_values = mask_words[:].rearrange("p w n u -> p (w n u)").bitcast(BF16)
+            state["mask_words", g] = mask_words
 
+        def regroup_b(g):
+            b_nat = state["loads", g][3]
             b_grouped = grouped.tile([P, CH, NJ * PACK], BF16, align_bytes=64)
             b_target = b_grouped[:].rearrange("p d (j t) -> p j d t", t=PACK)
             b_source = b_nat[:].rearrange("p t j d -> p j d t")
@@ -138,61 +136,112 @@ def tile_trianglemultiplicativeupdate_pa_k_kernel(
                     op0=ALU.mult,
                     op1=ALU.add,
                 )
+            state["b_grouped", g] = b_grouped
 
+        def mask(g, name, side):
+            values = state["mask_words", g][:, side, :, :].rearrange("p n u -> p (n u)").bitcast(BF16)
+            rows = state[name, g]
             nc.vector.tensor_tensor(
-                out=a_grouped[:],
-                in0=a_grouped[:],
-                in1=mask_values[:, : NI * PACK].unsqueeze(1).to_broadcast([P, CH, NI * PACK]),
+                out=rows[:],
+                in0=rows[:],
+                in1=values.unsqueeze(1).to_broadcast([P, CH, NI * PACK]),
                 op=ALU.mult,
             )
-            nc.vector.tensor_tensor(
-                out=b_grouped[:],
-                in0=b_grouped[:],
-                in1=mask_values[:, NI * PACK :].unsqueeze(1).to_broadcast([P, CH, NJ * PACK]),
-                op=ALU.mult,
-            )
-            nc.vector.quantize_mx(
-                out=a_codes[:, c, :].bitcast(FP8X4),
-                scales=a_scales[:, c, :],
-                in_=a_grouped[:].rearrange("p d n -> p (d n)"),
-            )
-            nc.vector.quantize_mx(
-                out=b_codes[:, c, :].bitcast(FP8X4),
-                scales=b_scales[:, c, :],
-                in_=b_grouped[:].rearrange("p d n -> p (d n)"),
-            )
 
-        def multiply(r):
-            a_codes, a_scales, b_codes, b_scales = codes[r]
+        def quantise(g, halves):
+            if halves[0].start == 0:
+                a_codes = quant.tile([P, CH * NI], U32, align_bytes=64)
+                a_scales = quant.tile([P, CH * NI], U8, align_bytes=64)
+                b_codes = quant.tile([P, CH * NJ], U32, align_bytes=64)
+                b_scales = quant.tile([P, CH * NJ], U8, align_bytes=64)
+                state["codes", g] = (a_codes, a_scales, b_codes, b_scales)
+            a_codes, a_scales, b_codes, b_scales = state["codes", g]
+            for ch in halves:
+                cols = slice(ch.start * P, ch.stop * P)
+                nc.vector.quantize_mx(
+                    out=a_codes[:, cols].bitcast(FP8X4),
+                    scales=a_scales[:, cols],
+                    in_=state["a_grouped", g][:, ch, :].rearrange("p d n -> p (d n)"),
+                )
+                nc.vector.quantize_mx(
+                    out=b_codes[:, cols].bitcast(FP8X4),
+                    scales=b_scales[:, cols],
+                    in_=state["b_grouped", g][:, ch, :].rearrange("p d n -> p (d n)"),
+                )
+
+        def multiply(r, d):
+            first = sum(ROUNDS[:r])
+            h, s = divmod(d, HALF)
+            if s == 0:
+                state["acc", r, h] = acc_psum.tile([P, HALF, NJ], F32, name="acc", tag="acc%d" % h)
+            cols = slice(d * P, (d + 1) * P)
+            for c in range(ROUNDS[r]):
+                a_codes, a_scales, b_codes, b_scales = state["codes", first + c]
+                nc.tensor.matmul_mx(
+                    out=state["acc", r, h][:, s, :],
+                    lhsT=a_codes[:, cols].bitcast(FP8X4),
+                    lhsT_scale=a_scales[:, cols],
+                    rhs=b_codes[:, cols].bitcast(FP8X4),
+                    rhs_scale=b_scales[:, cols],
+                    start=(c == 0),
+                    stop=(c == ROUNDS[r] - 1),
+                )
+
+        def add_up(r, h):
+            ch = slice(h * HALF, (h + 1) * HALF)
+            acc = state["acc", r, h]
+            if r == 0:
+                nc.scalar.copy(out=x_sum[:, ch, :], in_=acc[:])
+            else:
+                nc.vector.tensor_tensor(
+                    out=x_sum[:, ch, :], in0=acc[:], in1=x_sum[:, ch, :], op=ALU.add
+                )
+
+        last_of = {}
+        for r in range(len(ROUNDS)):
+            last_of[sum(ROUNDS[: r + 1]) - 1] = r
+
+        with tc.manual_schedule():
+            load(0)
+            load(1)
+            turn_a(0, (0, 1))
+            turn_mask_b(0)
+            turn_a(0, (2, 3))
+            turn_mask_words(0)
+            regroup_b(0)
+            waiting = []
+            for g in range(PASSES):
+                if g + 2 < PASSES:
+                    load(g + 2)
+                if g == 0:
+                    nc.sync.dma_start(out=gain_bf[:], in_=ln_out_w.partition_broadcast(P))
+                    nc.sync.dma_start(out=bias_bf[:], in_=ln_out_b.partition_broadcast(P))
+                mask(g, "a_grouped", 0)
+                if g + 1 < PASSES:
+                    turn_mask_b(g + 1)
+                    turn_a(g + 1, (0, 1))
+                    turn_mask_words(g + 1)
+                    turn_a(g + 1, (2, 3))
+                    regroup_b(g + 1)
+                mask(g, "b_grouped", 1)
+                issued = waiting[:2] if g < PASSES - 1 else waiting
+                waiting = waiting[len(issued) :]
+                for r, d in issued:
+                    multiply(r, d)
+                    if d % HALF == HALF - 1:
+                        add_up(r, d // HALF)
+                if g < PASSES - 1:
+                    quantise(g, (slice(0, CH),))
+                if g in last_of:
+                    waiting.extend((last_of[g], d) for d in range(CH))
+                if g == 1:
+                    nc.gpsimd.tensor_copy(out=gain[:], in_=gain_bf[:])
+                    nc.gpsimd.tensor_copy(out=bias[:], in_=bias_bf[:])
             for h in range(CH // HALF):
-                ch = slice(h * HALF, (h + 1) * HALF)
-                acc = acc_psum.tile([P, HALF, NJ], F32, tag="acc%d" % h)
-                for s in range(HALF):
-                    cols = slice((h * HALF + s) * P, (h * HALF + s + 1) * P)
-                    for c in range(ROUND):
-                        nc.tensor.matmul_mx(
-                            out=acc[:, s, :],
-                            lhsT=a_codes[:, c, cols].bitcast(FP8X4),
-                            lhsT_scale=a_scales[:, c, cols],
-                            rhs=b_codes[:, c, cols].bitcast(FP8X4),
-                            rhs_scale=b_scales[:, c, cols],
-                            start=(c == 0),
-                            stop=(c == ROUND - 1),
-                        )
-                if r == 0:
-                    nc.scalar.copy(out=x_sum[:, ch, :], in_=acc[:])
-                elif r < ROUNDS - 1:
-                    nc.vector.tensor_tensor(
-                        out=x_sum[:, ch, :], in0=acc[:], in1=x_sum[:, ch, :], op=ALU.add
-                    )
-                else:
-                    last_acc.append(acc)
-
-        for g in range(PASSES):
-            prepare_and_quantise(g)
-            if g >= ROUND + LAG - 1 and (g - LAG + 1) % ROUND == 0:
-                multiply((g - LAG + 1) // ROUND - 1)
-        multiply(ROUNDS - 1)
+                quantise(PASSES - 1, (slice(h * HALF, (h + 1) * HALF),))
+                for r, d in waiting[h * HALF : (h + 1) * HALF]:
+                    multiply(r, d)
+        last_acc = [state["acc", len(ROUNDS) - 1, h] for h in range(CH // HALF)]
 
         x = norm.tile([P, NJ, CH], F32)
         total = norm.tile([P, NJ], F32)
@@ -203,15 +252,15 @@ def tile_trianglemultiplicativeupdate_pa_k_kernel(
         std = norm.tile([P, NJ], F32)
         rstd = norm.tile([P, NJ], F32)
         y = norm.tile([P, NJ, CH], F32)
+        for h in range(CH // HALF):
+            ch = slice(h * HALF, (h + 1) * HALF)
+            nc.vector.tensor_tensor(
+                out=x[:, :, ch],
+                in0=last_acc[h][:].rearrange("p d j -> p j d"),
+                in1=x_sum[:, ch, :].rearrange("p d j -> p j d"),
+                op=ALU.add,
+            )
         for js in (slice(0, J_HALF), slice(J_HALF, NJ)):
-            for h in range(CH // HALF):
-                ch = slice(h * HALF, (h + 1) * HALF)
-                nc.vector.tensor_tensor(
-                    out=x[:, js, ch],
-                    in0=last_acc[h][:, :, js].rearrange("p d j -> p j d"),
-                    in1=x_sum[:, ch, js].rearrange("p d j -> p j d"),
-                    op=ALU.add,
-                )
             nc.vector.tensor_reduce(
                 out=total[:, js], in_=x[:, js, :], axis=mybir.AxisListType.X, op=ALU.add
             )
@@ -243,7 +292,8 @@ def tile_trianglemultiplicativeupdate_pa_k_kernel(
                 in1=rstd[:, js].unsqueeze(2).to_broadcast([P, J_HALF, CH]),
                 op=ALU.mult,
             )
-            nc.vector.tensor_tensor(
+            add_bias = nc.gpsimd if js.start == 0 else nc.vector
+            add_bias.tensor_tensor(
                 out=y[:, js, :],
                 in0=y[:, js, :],
                 in1=bias[:].unsqueeze(1).to_broadcast([P, J_HALF, CH]),

@@ -22,7 +22,8 @@ PASSES = NK // K_PASS
 ROUNDS = (6, 5, 4, 1)
 PAIRS = CH // 2
 HALF = CH // 2
-J_SCALAR = 40
+J_SCALAR = 44
+FIRST_TAGS = ("x", "centred", "squares", "weighted")
 J_HALF = NJ // 2
 EPS = 1e-5
 
@@ -88,6 +89,14 @@ def tile_trianglemultiplicativeupdate_pa_k_kernel(
             nc.scalar.copy(out=mask_b_rows_j[:], in_=mask_b_turned[:].rearrange("p n k -> p (n k)"))
             state["mask_b_rows_j", g] = mask_b_rows_j
 
+        def split_first_a():
+            a_nat = state["loads", 0][2]
+            a_f32 = a_nat[:].bitcast(F32).rearrange("p (u q e w) -> p u e q w", u=2, e=2, w=PAIRS)
+            for w in range(PAIRS):
+                first_a = norm.tile([P, 2, 2, P], F32, name="first_a", tag=FIRST_TAGS[w])
+                nc.vector.tensor_copy(out=first_a[:], in_=a_f32[:, :, :, :, w])
+                state["first_a", w] = first_a
+
         def turn_a(g, pairs):
             a_nat = state["loads", g][2]
             a_f32 = a_nat[:].bitcast(F32).rearrange("p (u q e w) -> p u e q w", u=2, e=2, w=PAIRS)
@@ -97,10 +106,11 @@ def tile_trianglemultiplicativeupdate_pa_k_kernel(
                 )
             a_grouped = state["a_grouped", g]
             for w in pairs:
+                words = a_f32[:, :, :, :, w] if g > 0 else state["first_a", w][:]
                 turned = turn_psum.tile([P, PACK * NI], F32)
                 for t in range(PACK):
                     nc.tensor.transpose(
-                        turned[:, t * NI : (t + 1) * NI], a_f32[:, t // 2, t % 2, :, w], ident[:]
+                        turned[:, t * NI : (t + 1) * NI], words[:, t // 2, t % 2, :], ident[:]
                     )
                 copy = nc.vector.tensor_copy if g == 0 and w % 2 == 1 else nc.scalar.copy
                 copy(
@@ -204,6 +214,7 @@ def tile_trianglemultiplicativeupdate_pa_k_kernel(
         with tc.manual_schedule():
             load(0)
             load(1)
+            split_first_a()
             turn_a(0, (0, 1))
             turn_mask_b(0)
             turn_a(0, (2, 3))

from contextlib import ExitStack

import concourse.mybir as mybir
from concourse.masks import make_identity

F32 = mybir.dt.float32
BF16 = mybir.dt.bfloat16
U32 = mybir.dt.uint32
U8 = mybir.dt.uint8
FP8X4 = mybir.dt.float8_e4m3fn_x4
ALU = mybir.AluOpType
ACT = mybir.ActivationFunctionType

P = 128
NI = 128
NJ = 128
NK = 8192
CH = 8
PACK = 4
K_PASS = P * PACK
PASSES = NK // K_PASS
ROUNDS = (6, 5, 4, 1)
PAIRS = CH // 2
HALF = CH // 2
J_SCALAR = 44
FIRST_TAGS = ("x", "centred", "squares", "weighted")
J_HALF = NJ // 2
EPS = 1e-5

FLOPS = 2 * NI * NJ * NK * CH


def tile_trianglemultiplicativeupdate_pa_k_kernel(
    tc, a_gated, b_gated, mask_ik, mask_kj, ln_out_w, ln_out_b, out
):
    nc = tc.nc
    a_rows = a_gated[0].rearrange("i (g k) d -> g i (k d)", k=K_PASS)
    b_rows = b_gated[0].rearrange("(g u q e) j d -> g q u (e j d)", u=2, q=P, e=2)
    mask_a_rows = mask_ik[0].rearrange("i (g k) -> g i k", k=K_PASS)
    mask_b_rows = mask_kj[0].rearrange("(g n p) j -> g p n j", n=PACK, p=P)

    with ExitStack() as ctx:
        const = ctx.enter_context(tc.tile_pool(name="const", bufs=1))
        mask_pool = ctx.enter_context(tc.tile_pool(name="mask_pool", bufs=3))
        loads = ctx.enter_context(tc.tile_pool(name="loads", bufs=3))
        grouped = ctx.enter_context(tc.tile_pool(name="grouped", bufs=2))
        quant = ctx.enter_context(tc.tile_pool(name="quant", bufs=11))
        norm = ctx.enter_context(tc.tile_pool(name="norm", bufs=1))
        turn_psum = ctx.enter_context(tc.psum_pool(name="turn_psum", bufs=3))
        mask_turn_psum = ctx.enter_context(tc.psum_pool(name="mask_turn_psum", bufs=1))
        mask_psum = ctx.enter_context(tc.psum_pool(name="mask_psum", bufs=2))
        acc_psum = ctx.enter_context(tc.psum_pool(name="acc_psum", bufs=1))

        ident = const.tile([P, P], F32)
        make_identity(nc, ident[:])
        ident_bf = const.tile([P, P], BF16)
        make_identity(nc, ident_bf[:])
        eps_col = const.tile([P, 1], F32)
        nc.vector.memset(eps_col[:], EPS)
        warm = const.tile([P, 1], F32)
        nc.scalar.activation(out=warm[:], in_=eps_col[:], func=ACT.Sqrt)
        gain_bf = const.tile([P, CH], BF16)
        bias_bf = const.tile([P, CH], BF16)
        gain = const.tile([P, CH], F32)
        bias = const.tile([P, CH], F32)

        x_sum = const.tile([P, CH, NJ], F32)
        state = {}

        def load(g):
            a_nat = loads.tile([P, K_PASS * CH], BF16)
            nc.sync.dma_start(out=a_nat[:], in_=a_rows[g])
            mask_b = mask_pool.tile([P, PACK, NJ], BF16)
            nc.sync.dma_start(out=mask_b[:], in_=mask_b_rows[g])
            mask_a = mask_pool.tile([P, K_PASS], BF16)
            nc.sync.dma_start(out=mask_a[:], in_=mask_a_rows[g])
            b_nat = loads.tile([P, PACK, NJ, CH], BF16)
            nc.sync.dma_start(
                out=b_nat[:].rearrange("p (u e) j d -> p u (e j d)", u=2), in_=b_rows[g]
            )
            state["loads", g] = (mask_a, mask_b, a_nat, b_nat)

        def turn_mask_b(g):
            mask_b = state["loads", g][1]
            mask_b_turned = mask_turn_psum.tile([P, PACK, P], BF16)
            for n in range(PACK):
                nc.tensor.transpose(mask_b_turned[:, n, :], mask_b[:, n, :], ident_bf[:])
            mask_b_rows_j = mask_pool.tile([P, K_PASS], BF16)
            nc.scalar.copy(out=mask_b_rows_j[:], in_=mask_b_turned[:].rearrange("p n k -> p (n k)"))
            state["mask_b_rows_j", g] = mask_b_rows_j

        def split_first_a():
            a_nat = state["loads", 0][2]
            a_f32 = a_nat[:].bitcast(F32).rearrange("p (u q e w) -> p u e q w", u=2, e=2, w=PAIRS)
            for w in range(PAIRS):
                first_a = norm.tile([P, 2, 2, P], F32, name="first_a", tag=FIRST_TAGS[w])
                nc.vector.tensor_copy(out=first_a[:], in_=a_f32[:, :, :, :, w])
                state["first_a", w] = first_a

        def turn_a(g, pairs):
            a_nat = state["loads", g][2]
            a_f32 = a_nat[:].bitcast(F32).rearrange("p (u q e w) -> p u e q w", u=2, e=2, w=PAIRS)
            if pairs[0] == 0:
                state["a_grouped", g] = grouped.tile(
                    [P, CH, NI * PACK], BF16, name="a_grouped", align_bytes=64
                )
            a_grouped = state["a_grouped", g]
            for w in pairs:
                words = a_f32[:, :, :, :, w] if g > 0 else state["first_a", w][:]
                turned = turn_psum.tile([P, PACK * NI], F32)
                for t in range(PACK):
                    nc.tensor.transpose(
                        turned[:, t * NI : (t + 1) * NI], words[:, t // 2, t % 2, :], ident[:]
                    )
                copy = nc.vector.tensor_copy if g == 0 and w % 2 == 1 else nc.scalar.copy
                copy(
                    out=a_grouped[:, 2 * w : 2 * w + 2, :].rearrange("p s (i t) -> p s i t", t=PACK),
                    in_=turned[:].bitcast(BF16).rearrange("p (t i s) -> p s i t", t=PACK, s=2),
                )

        def turn_mask_words(g):
            mask_a = state["loads", g][0]
            mask_b_rows_j = state["mask_b_rows_j", g]
            mask_words = mask_psum.tile([P, 2, P, 2], F32)
            for u in range(2):
                half = slice(u * P, (u + 1) * P)
                nc.tensor.transpose(mask_words[:, 0, :, u], mask_a[:].bitcast(F32)[:, half], ident[:])
                nc.tensor.transpose(
                    mask_words[:, 1, :, u], mask_b_rows_j[:].bitcast(F32)[:, half], ident[:]
                )
            state["mask_words", g] = mask_words

        def regroup_b(g):
            b_nat = state["loads", g][3]
            b_grouped = grouped.tile([P, CH, NJ * PACK], BF16, align_bytes=64)
            b_target = b_grouped[:].rearrange("p d (j t) -> p j d t", t=PACK)
            b_source = b_nat[:].rearrange("p t j d -> p j d t")
            for h in range(CH // HALF):
                ch = slice(h * HALF, (h + 1) * HALF)
                nc.scalar.copy(out=b_target[:, :J_SCALAR, ch, :], in_=b_source[:, :J_SCALAR, ch, :])
                nc.gpsimd.tensor_scalar(
                    out=b_target[:, J_SCALAR:, ch, :],
                    in0=b_source[:, J_SCALAR:, ch, :],
                    scalar1=1.0,
                    scalar2=0.0,
                    op0=ALU.mult,
                    op1=ALU.add,
                )
            state["b_grouped", g] = b_grouped

        def mask(g, name, side):
            values = state["mask_words", g][:, side, :, :].rearrange("p n u -> p (n u)").bitcast(BF16)
            rows = state[name, g]
            nc.vector.tensor_tensor(
                out=rows[:],
                in0=rows[:],
                in1=values.unsqueeze(1).to_broadcast([P, CH, NI * PACK]),
                op=ALU.mult,
            )

        def quantise(g, halves):
            if halves[0].start == 0:
                a_codes = quant.tile([P, CH * NI], U32, align_bytes=64)
                a_scales = quant.tile([P, CH * NI], U8, align_bytes=64)
                b_codes = quant.tile([P, CH * NJ], U32, align_bytes=64)
                b_scales = quant.tile([P, CH * NJ], U8, align_bytes=64)
                state["codes", g] = (a_codes, a_scales, b_codes, b_scales)
            a_codes, a_scales, b_codes, b_scales = state["codes", g]
            for ch in halves:
                cols = slice(ch.start * P, ch.stop * P)
                nc.vector.quantize_mx(
                    out=a_codes[:, cols].bitcast(FP8X4),
                    scales=a_scales[:, cols],
                    in_=state["a_grouped", g][:, ch, :].rearrange("p d n -> p (d n)"),
                )
                nc.vector.quantize_mx(
                    out=b_codes[:, cols].bitcast(FP8X4),
                    scales=b_scales[:, cols],
                    in_=state["b_grouped", g][:, ch, :].rearrange("p d n -> p (d n)"),
                )

        def multiply(r, d):
            first = sum(ROUNDS[:r])
            h, s = divmod(d, HALF)
            if s == 0:
                state["acc", r, h] = acc_psum.tile([P, HALF, NJ], F32, name="acc", tag="acc%d" % h)
            cols = slice(d * P, (d + 1) * P)
            for c in range(ROUNDS[r]):
                a_codes, a_scales, b_codes, b_scales = state["codes", first + c]
                nc.tensor.matmul_mx(
                    out=state["acc", r, h][:, s, :],
                    lhsT=a_codes[:, cols].bitcast(FP8X4),
                    lhsT_scale=a_scales[:, cols],
                    rhs=b_codes[:, cols].bitcast(FP8X4),
                    rhs_scale=b_scales[:, cols],
                    start=(c == 0),
                    stop=(c == ROUNDS[r] - 1),
                )

        def add_up(r, h):
            ch = slice(h * HALF, (h + 1) * HALF)
            acc = state["acc", r, h]
            if r == 0:
                nc.scalar.copy(out=x_sum[:, ch, :], in_=acc[:])
            else:
                nc.vector.tensor_tensor(
                    out=x_sum[:, ch, :], in0=acc[:], in1=x_sum[:, ch, :], op=ALU.add
                )

        last_of = {}
        for r in range(len(ROUNDS)):
            last_of[sum(ROUNDS[: r + 1]) - 1] = r

        with tc.manual_schedule():
            load(0)
            load(1)
            split_first_a()
            turn_a(0, (0, 1))
            turn_mask_b(0)
            turn_a(0, (2, 3))
            turn_mask_words(0)
            regroup_b(0)
            waiting = []
            for g in range(PASSES):
                if g + 2 < PASSES:
                    load(g + 2)
                if g == 0:
                    nc.sync.dma_start(out=gain_bf[:], in_=ln_out_w.partition_broadcast(P))
                    nc.sync.dma_start(out=bias_bf[:], in_=ln_out_b.partition_broadcast(P))
                mask(g, "a_grouped", 0)
                if g + 1 < PASSES:
                    turn_mask_b(g + 1)
                    turn_a(g + 1, (0, 1))
                    turn_mask_words(g + 1)
                    turn_a(g + 1, (2, 3))
                    regroup_b(g + 1)
                mask(g, "b_grouped", 1)
                issued = waiting[:2] if g < PASSES - 1 else waiting
                waiting = waiting[len(issued) :]
                for r, d in issued:
                    multiply(r, d)
                    if d % HALF == HALF - 1:
                        add_up(r, d // HALF)
                if g < PASSES - 1:
                    quantise(g, (slice(0, CH),))
                if g in last_of:
                    waiting.extend((last_of[g], d) for d in range(CH))
                if g == 1:
                    nc.gpsimd.tensor_copy(out=gain[:], in_=gain_bf[:])
                    nc.gpsimd.tensor_copy(out=bias[:], in_=bias_bf[:])
            for h in range(CH // HALF):
                quantise(PASSES - 1, (slice(h * HALF, (h + 1) * HALF),))
                for r, d in waiting[h * HALF : (h + 1) * HALF]:
                    multiply(r, d)
        last_acc = [state["acc", len(ROUNDS) - 1, h] for h in range(CH // HALF)]

        x = norm.tile([P, NJ, CH], F32)
        total = norm.tile([P, NJ], F32)
        centred = norm.tile([P, NJ, CH], F32)
        squares = norm.tile([P, NJ, CH], F32)
        weighted = norm.tile([P, NJ, CH], F32)
        spread = norm.tile([P, NJ], F32)
        std = norm.tile([P, NJ], F32)
        rstd = norm.tile([P, NJ], F32)
        y = norm.tile([P, NJ, CH], F32)
        for h in range(CH // HALF):
            ch = slice(h * HALF, (h + 1) * HALF)
            nc.vector.tensor_tensor(
                out=x[:, :, ch],
                in0=last_acc[h][:].rearrange("p d j -> p j d"),
                in1=x_sum[:, ch, :].rearrange("p d j -> p j d"),
                op=ALU.add,
            )
        for js in (slice(0, J_HALF), slice(J_HALF, NJ)):
            nc.vector.tensor_reduce(
                out=total[:, js], in_=x[:, js, :], axis=mybir.AxisListType.X, op=ALU.add
            )
            nc.vector.scalar_tensor_tensor(
                out=centred[:, js, :],
                in0=total[:, js].unsqueeze(2).to_broadcast([P, J_HALF, CH]),
                scalar=-1.0 / CH,
                in1=x[:, js, :],
                op0=ALU.mult,
                op1=ALU.add,
            )
            nc.scalar.activation(out=squares[:, js, :], in_=centred[:, js, :], func=ACT.Square)
            nc.gpsimd.tensor_tensor(
                out=weighted[:, js, :],
                in0=centred[:, js, :],
                in1=gain[:].unsqueeze(1).to_broadcast([P, J_HALF, CH]),
                op=ALU.mult,
            )
            nc.vector.tensor_reduce(
                out=spread[:, js], in_=squares[:, js, :], axis=mybir.AxisListType.X, op=ALU.add
            )
            nc.scalar.activation(
                out=std[:, js], in_=spread[:, js], func=ACT.Sqrt, bias=eps_col[:], scale=1.0 / CH
            )
            nc.vector.reciprocal(out=rstd[:, js], in_=std[:, js])
            nc.vector.tensor_tensor(
                out=y[:, js, :],
                in0=weighted[:, js, :],
                in1=rstd[:, js].unsqueeze(2).to_broadcast([P, J_HALF, CH]),
                op=ALU.mult,
            )
            add_bias = nc.gpsimd if js.start == 0 else nc.vector
            add_bias.tensor_tensor(
                out=y[:, js, :],
                in0=y[:, js, :],
                in1=bias[:].unsqueeze(1).to_broadcast([P, J_HALF, CH]),
                op=ALU.add,
            )
            nc.sync.dma_start(out=out[0][:, js, :], in_=y[:, js, :])
